import numpy as np
import ml_dtypes


def mxq(x, axis, fmt="e4m3"):
    dtype, down = {"e4m3": (ml_dtypes.float8_e4m3fn, 7), "e5m2": (ml_dtypes.float8_e5m2, 14)}[fmt]
    v = np.moveaxis(np.asarray(x, np.float32).astype(ml_dtypes.bfloat16).astype(np.float64), axis, -1)
    blocks = v.reshape(v.shape[:-1] + (-1, 32))
    amax = np.abs(blocks).max(-1, keepdims=True)
    byte = np.maximum(np.where(amax > 0, np.frexp(amax)[1] - 1 + 127, 0) - down, 1)
    scale = np.exp2(byte - 127.0)
    codes = (blocks / scale).astype(np.float32).astype(dtype).astype(np.float64)
    return np.moveaxis((codes * scale).reshape(v.shape), -1, axis)


WIDE = False


def mx_kscale(k):
    if not WIDE:
        return np.ones(k)
    levels = np.array([10, -10, 5, -5, 0])
    if k % 512:
        return np.exp2(np.random.permutation(np.resize(levels, k // 32))).repeat(32)
    a = np.empty((k // 512, 16))
    for p in range(k // 512):
        a[p, :8] = np.random.permutation(np.resize(levels, 8))
        for g in range(8):
            far = levels[np.abs(levels - a[p, g]) >= 10]
            a[p, g + 8] = far[np.random.randint(len(far))]
    return np.exp2(a.ravel()).repeat(32)


BF16 = ml_dtypes.bfloat16


def bf(x):
    return np.asarray(x, np.float32).astype(BF16)


def f64(x):
    return np.asarray(x).astype(np.float64)


B, S, IN, OUT, A, R = 8, 128, 2048, 2048, 8, 128
G = B // A
SCALING = 2.0


def setup_inputs():
    s = mx_kscale(IN)
    return {"data": bf(np.random.standard_normal((B, S, IN)) * s),
            "W": bf(np.random.standard_normal((OUT, IN)) / np.sqrt(IN) / s),
            "t_lora": bf(np.random.standard_normal((A, G, S, R))),
            "lora_b": bf(np.random.standard_normal((A, OUT, R)) * 0.5 / np.sqrt(R))}


def core(data, W, t_lora, lora_b):
    base = mxq(f64(data), 2, "e4m3") @ mxq(f64(W), 1, "e4m3").T
    delta = (f64(t_lora).reshape(A, G * S, R) @ f64(lora_b).transpose(0, 2, 1)) * SCALING
    return base + delta.reshape(B, S, OUT)


def e4m3fn_bytes(y):
    return np.clip(np.asarray(y, np.float64), -448.0, 448.0).astype(np.float32).astype(ml_dtypes.float8_e4m3fn).view(np.uint8)


Y_SCALE = 150.0


def reference(data, W, t_lora, lora_b):
    out = core(data, W, t_lora, lora_b)
    return out, e4m3fn_bytes(out * Y_SCALE)

@@ -1,0 +1,238 @@
+from contextlib import ExitStack
+
+import concourse.mybir as mybir
+from concourse.masks import make_identity
+
+B, S, IN, OUT, R = 8, 128, 2048, 2048, 128
+FLOPS = 2 * B * S * OUT * IN + 2 * B * S * OUT * R
+
+F32 = mybir.dt.float32
+BF16 = mybir.dt.bfloat16
+U32 = mybir.dt.uint32
+U8 = mybir.dt.uint8
+FP8X4 = mybir.dt.float8_e4m3fn_x4
+FP8 = mybir.dt.float8_e4m3fn
+ACT = mybir.ActivationFunctionType
+ALU = mybir.AluOpType
+
+P = 128
+NT = 512
+PASSES = IN // 512
+SLOTS = 16
+
+RAW_BUFS = 10
+PRECOPY = ()
+V_EVAC = ("d0", "d1", "d2", "d3", "d4", "d5", "d6", "d7", "w0", "w1", "w2", "w3")
+
+
+def tile_linear_pa_kernel(tc, data, W, t_lora, lora_b, out_0, out_1):
+    nc = tc.nc
+    with ExitStack() as ctx:
+        const = ctx.enter_context(tc.tile_pool(name="const", bufs=1))
+        rawp = ctx.enter_context(tc.tile_pool(name="rawp", bufs=RAW_BUFS))
+        pcp = ctx.enter_context(tc.tile_pool(name="pcp", bufs=3))
+        grpp = ctx.enter_context(tc.tile_pool(name="grpp", bufs=4))
+        codes = ctx.enter_context(tc.tile_pool(name="codes", bufs=1))
+        lbrp = ctx.enter_context(tc.tile_pool(name="lbrp", bufs=4))
+        lbtp = ctx.enter_context(tc.tile_pool(name="lbtp", bufs=4))
+        lsbp = ctx.enter_context(tc.tile_pool(name="lsbp", bufs=6))
+        o0p = ctx.enter_context(tc.tile_pool(name="o0p", bufs=4))
+        psum = ctx.enter_context(tc.psum_pool(name="psum", bufs=8))
+        ctx.enter_context(tc.manual_schedule(engines={mybir.EngineType.PE}))
+
+        ident_f = const.tile([P, P], F32, name="ident_f")
+        make_identity(nc, ident_f[:])
+        ident_b = const.tile([P, P], BF16, name="ident_b")
+        make_identity(nc, ident_b[:])
+        warm = const.tile([P, 2], F32, name="warm")
+        nc.vector.memset(warm[:], 0.0)
+        nc.scalar.activation(out=warm[:, 1:2], in_=warm[:, 0:1], func=ACT.Copy, scale=2.0)
+
+        tl = const.tile([P, B, R], BF16, name="tl")
+        tT = const.tile([P, B, S], BF16, name="tT")
+        dc = [codes.tile([P, 512], U32, name="dc%d" % b, align_bytes=64) for b in range(B)]
+        ds = [codes.tile([P, 512], U8, name="ds%d" % b, align_bytes=64) for b in range(B)]
+        wc = [codes.tile([P, PASSES, NT], U32, name="wc%d" % n, align_bytes=64) for n in range(4)]
+        ws = [codes.tile([P, PASSES, NT], U8, name="ws%d" % n, align_bytes=64) for n in range(4)]
+        o1 = [codes.tile([P, OUT], FP8, name="o1_%d" % b) for b in range(B)]
+
+        raw = {}
+        lbraw = {}
+        lbT = {}
+        lsb = {}
+
+        def load(key):
+            i = int(key[1:])
+            t = rawp.tile([P, IN], BF16, tag="raw", name="raw_" + key)
+            if key[0] == "d":
+                nc.sync.dma_start(out=t[:], in_=data[i])
+            else:
+                nc.sync.dma_start(out=t[:], in_=W[P * i : P * (i + 1), :])
+            raw[key] = t
+
+        def load_lb(l):
+            n, a2 = l // 4, l % 4
+            t = lbrp.tile([P, 2, NT], BF16, tag="lbraw", name="lbraw%d" % l)
+            nc.sync.dma_start(
+                out=t[:],
+                in_=lora_b[2 * a2 : 2 * a2 + 2, NT * n : NT * (n + 1), :].rearrange("a (p t) r -> p a (t r)", t=4),
+            )
+            lbraw[l] = t
+
+        def precopy(key):
+            if key not in PRECOPY:
+                return
+            pc = pcp.tile([P, IN // 2], F32, tag="pc", name="pc_" + key)
+            nc.vector.tensor_copy(
+                out=pc[:].rearrange("p (g u w) -> p g u w", g=PASSES, u=2),
+                in_=raw[key][:].bitcast(F32).rearrange("p (g w u) -> p g u w", g=PASSES, u=2),
+            )
+            raw[key] = pc
+
+        def xpose(key):
+            i = int(key[1:])
+            if key in PRECOPY:
+                words = raw[key][:]
+            else:
+                words = raw[key][:].bitcast(F32)
+            grp = grpp.tile([P, IN], BF16, tag="grp", name="grp_" + key, align_bytes=64)
+            grp_w = grp[:].bitcast(F32)
+            for h in range(2):
+                bank = psum.tile([P, 512], F32, tag="bank", name="xt_%s_%d" % (key, h))
+                for g2 in range(2):
+                    g = 2 * h + g2
+                    for u in range(2):
+                        if key in PRECOPY:
+                            src = words[:, 256 * g + 128 * u : 256 * g + 128 * (u + 1)]
+                        else:
+                            src = words[:, 256 * g + u : 256 * (g + 1) : 2]
+                        c = 128 * (2 * g2 + u)
+                        nc.tensor.transpose(bank[:, c : c + 128], src, ident_f[:])
+                src = bank[:].rearrange("p (g u r) -> p g r u", g=2, u=2)
+                dst = grp_w[:, 512 * h : 512 * (h + 1)].rearrange("p (g r u) -> p g r u", g=2, u=2)
+                if h == 1 and key in V_EVAC:
+                    nc.vector.tensor_copy(out=dst, in_=src)
+                else:
+                    nc.scalar.copy(out=dst, in_=src)
+            if key[0] == "d":
+                nc.vector.quantize_mx(out=dc[i][:].bitcast(FP8X4), scales=ds[i][:], in_=grp[:])
+            else:
+                n, j = i // 4, i % 4
+                for g in range(PASSES):
+                    nc.vector.quantize_mx(
+                        out=wc[n][:, g, P * j : P * (j + 1)].bitcast(FP8X4),
+                        scales=ws[n][:, g, P * j : P * (j + 1)],
+                        in_=grp[:, 512 * g : 512 * (g + 1)],
+                    )
+
+        def xpose_tl():
+            bank = psum.tile([P, 1024], BF16, tag="bank", name="tlT")
+            for a in range(B):
+                nc.tensor.transpose(bank[:, S * a : S * (a + 1)], tl[:, a, :], ident_b[:])
+            nc.vector.tensor_copy(out=tT[:].rearrange("p a s -> p (a s)"), in_=bank[:])
+
+        def xpose_lb(l):
+            bank = psum.tile([P, 1024], BF16, tag="bank", name="lbx%d" % l)
+            for a in range(2):
+                for t in range(4):
+                    c = 512 * a + 128 * t
+                    nc.tensor.transpose(bank[:, c : c + 128], lbraw[l][:, a, 128 * t : 128 * (t + 1)], ident_b[:])
+            t_sb = lbtp.tile([P, 2, NT], BF16, tag="lbT", name="lbT%d" % l)
+            nc.scalar.copy(out=t_sb[:].rearrange("p a c -> p (a c)"), in_=bank[:])
+            lbT[l] = t_sb
+
+        def lora_mm(s):
+            n = s // 4
+            for e in range(2):
+                b = 2 * (s % 4) + e
+                lp = psum.tile([P, NT], F32, tag="bank", name="lp%d_%d" % (b, n))
+                nc.tensor.matmul(lp[:], lhsT=tT[:, b, :], rhs=lbT[s][:, e, :], start=True, stop=True)
+                t_sb = lsbp.tile([P, NT], F32, tag="lsb", name="lsb%d_%d" % (b, n))
+                nc.scalar.activation(
+                    out=t_sb[:].rearrange("s (p t) -> s p t", t=4),
+                    in_=lp[:].rearrange("s (t p) -> s p t", t=4),
+                    func=ACT.Copy,
+                    scale=2.0,
+                )
+                lsb[(b, n)] = t_sb
+
+        def mx_mm(s):
+            n = s // 4
+            for e in range(2):
+                b = 2 * (s % 4) + e
+                acc = psum.tile([P, NT], F32, tag="bank", name="acc%d_%d" % (b, n))
+                for g in range(PASSES):
+                    nc.tensor.matmul_mx(
+                        out=acc[:],
+                        lhsT=dc[b][:, P * g : P * (g + 1)].bitcast(FP8X4),
+                        lhsT_scale=ds[b][:, P * g : P * (g + 1)],
+                        rhs=wc[n][:, g, :].bitcast(FP8X4),
+                        rhs_scale=ws[n][:, g, :],
+                        start=(g == 0),
+                        stop=(g == PASSES - 1),
+                    )
+                o0 = o0p.tile([P, NT], F32, tag="o0", name="o0_%d_%d" % (b, n))
+                nc.vector.tensor_tensor(out=o0[:], in0=acc[:], in1=lsb[(b, n)][:], op=ALU.add)
+                nc.sync.dma_start(out=out_0[b, :, NT * n : NT * (n + 1)], in_=o0[:])
+                nc.vector.tensor_scalar(
+                    out=o1[b][:, NT * n : NT * (n + 1)],
+                    in0=o0[:],
+                    scalar1=150.0,
+                    scalar2=None,
+                    op0=ALU.mult,
+                    saturate=False,
+                )
+                if n == 3:
+                    nc.sync.dma_start(out=out_1[b], in_=o1[b][:].bitcast(U8))
+
+        def slot_tiles(s):
+            keys = []
+            if s <= 2:
+                keys = ["d%d" % (2 * s + 2), "d%d" % (2 * s + 3)]
+            if s <= 11:
+                keys.append("w%d" % (4 + s))
+            return keys
+
+        def slot_loads(s):
+            if s >= SLOTS:
+                return
+            keys = slot_tiles(s)
+            for key in keys[:-1]:
+                load(key)
+            if s + 1 < SLOTS:
+                load_lb(s + 1)
+            for key in keys[-1:]:
+                load(key)
+
+        for key in ("d0", "w0", "w1", "w2", "w3"):
+            load(key)
+        nc.sync.dma_start(out=tl[:], in_=t_lora.rearrange("a g s r -> s (a g) r"))
+        load_lb(0)
+        load("d1")
+        slot_loads(0)
+        slot_loads(1)
+        for key in ("d0", "w0", "w1", "w2", "w3"):
+            precopy(key)
+            xpose(key)
+        xpose_tl()
+        xpose_lb(0)
+        precopy("d1")
+        xpose("d1")
+        for key in slot_tiles(0):
+            precopy(key)
+        lora_mm(0)
+
+        for s in range(SLOTS):
+            slot_loads(s + 2)
+            for key in slot_tiles(s + 1):
+                precopy(key)
+            keys = slot_tiles(s)
+            for key in keys[:-1]:
+                xpose(key)
+            if s + 1 < SLOTS:
+                xpose_lb(s + 1)
+            for key in keys[-1:]:
+                xpose(key)
+            mx_mm(s)
+            if s + 1 < SLOTS:
+                lora_mm(s + 1)

@@ -20,8 +20,9 @@ NT = 512
 PASSES = IN // 512
 SLOTS = 16
 
-RAW_BUFS = 10
-PRECOPY = ()
+RAW_BUFS = 14
+LA = 3
+PRECOPY = ("w7", "w8", "w9", "w10", "w11", "w12", "w13", "w14", "w15")
 V_EVAC = ("d0", "d1", "d2", "d3", "d4", "d5", "d6", "d7", "w0", "w1", "w2", "w3")
 
 
@@ -33,12 +34,12 @@ def tile_linear_pa_kernel(tc, data, W, t_lora, lora_b, out_0, out_1):
         pcp = ctx.enter_context(tc.tile_pool(name="pcp", bufs=3))
         grpp = ctx.enter_context(tc.tile_pool(name="grpp", bufs=4))
         codes = ctx.enter_context(tc.tile_pool(name="codes", bufs=1))
-        lbrp = ctx.enter_context(tc.tile_pool(name="lbrp", bufs=4))
+        lbrp = ctx.enter_context(tc.tile_pool(name="lbrp", bufs=5))
         lbtp = ctx.enter_context(tc.tile_pool(name="lbtp", bufs=4))
         lsbp = ctx.enter_context(tc.tile_pool(name="lsbp", bufs=6))
         o0p = ctx.enter_context(tc.tile_pool(name="o0p", bufs=4))
         psum = ctx.enter_context(tc.psum_pool(name="psum", bufs=8))
-        ctx.enter_context(tc.manual_schedule(engines={mybir.EngineType.PE}))
+        ctx.enter_context(tc.manual_schedule(engines={mybir.EngineType.PE, mybir.EngineType.DVE, mybir.EngineType.Activation}))
 
         ident_f = const.tile([P, P], F32, name="ident_f")
         make_identity(nc, ident_f[:])
@@ -209,8 +210,8 @@ def tile_linear_pa_kernel(tc, data, W, t_lora, lora_b, out_0, out_1):
         nc.sync.dma_start(out=tl[:], in_=t_lora.rearrange("a g s r -> s (a g) r"))
         load_lb(0)
         load("d1")
-        slot_loads(0)
-        slot_loads(1)
+        for s in range(LA):
+            slot_loads(s)
         for key in ("d0", "w0", "w1", "w2", "w3"):
             precopy(key)
             xpose(key)
@@ -218,15 +219,13 @@ def tile_linear_pa_kernel(tc, data, W, t_lora, lora_b, out_0, out_1):
         xpose_lb(0)
         precopy("d1")
         xpose("d1")
-        for key in slot_tiles(0):
-            precopy(key)
         lora_mm(0)
 
         for s in range(SLOTS):
-            slot_loads(s + 2)
+            slot_loads(s + LA)
+            keys = slot_tiles(s)
             for key in slot_tiles(s + 1):
                 precopy(key)
-            keys = slot_tiles(s)
             for key in keys[:-1]:
                 xpose(key)
             if s + 1 < SLOTS:

@@ -21,7 +21,8 @@ PASSES = IN // 512
 SLOTS = 16
 
 RAW_BUFS = 14
-LA = 3
+GROUPS = ((0,), (1,), (2,), (3,), (4, 5), (6, 7), (8, 9), (10, 11), (12, 13), (14, 15))
+LA = 5
 PRECOPY = ("w7", "w8", "w9", "w10", "w11", "w12", "w13", "w14", "w15")
 V_EVAC = ("d0", "d1", "d2", "d3", "d4", "d5", "d6", "d7", "w0", "w1", "w2", "w3")
 
@@ -31,13 +32,13 @@ def tile_linear_pa_kernel(tc, data, W, t_lora, lora_b, out_0, out_1):
     with ExitStack() as ctx:
         const = ctx.enter_context(tc.tile_pool(name="const", bufs=1))
         rawp = ctx.enter_context(tc.tile_pool(name="rawp", bufs=RAW_BUFS))
-        pcp = ctx.enter_context(tc.tile_pool(name="pcp", bufs=3))
+        pcp = ctx.enter_context(tc.tile_pool(name="pcp", bufs=4))
         grpp = ctx.enter_context(tc.tile_pool(name="grpp", bufs=4))
         codes = ctx.enter_context(tc.tile_pool(name="codes", bufs=1))
-        lbrp = ctx.enter_context(tc.tile_pool(name="lbrp", bufs=5))
+        lbrp = ctx.enter_context(tc.tile_pool(name="lbrp", bufs=8))
         lbtp = ctx.enter_context(tc.tile_pool(name="lbtp", bufs=4))
-        lsbp = ctx.enter_context(tc.tile_pool(name="lsbp", bufs=6))
-        o0p = ctx.enter_context(tc.tile_pool(name="o0p", bufs=4))
+        lsbp = ctx.enter_context(tc.tile_pool(name="lsbp", bufs=10))
+        o0p = ctx.enter_context(tc.tile_pool(name="o0p", bufs=6))
         psum = ctx.enter_context(tc.psum_pool(name="psum", bufs=8))
         ctx.enter_context(tc.manual_schedule(engines={mybir.EngineType.PE, mybir.EngineType.DVE, mybir.EngineType.Activation}))
 
@@ -61,6 +62,7 @@ def tile_linear_pa_kernel(tc, data, W, t_lora, lora_b, out_0, out_1):
         lbraw = {}
         lbT = {}
         lsb = {}
+        grps = {}
 
         def load(key):
             i = int(key[1:])
@@ -90,8 +92,7 @@ def tile_linear_pa_kernel(tc, data, W, t_lora, lora_b, out_0, out_1):
             )
             raw[key] = pc
 
-        def xpose(key):
-            i = int(key[1:])
+        def x_t(key):
             if key in PRECOPY:
                 words = raw[key][:]
             else:
@@ -115,6 +116,11 @@ def tile_linear_pa_kernel(tc, data, W, t_lora, lora_b, out_0, out_1):
                     nc.vector.tensor_copy(out=dst, in_=src)
                 else:
                     nc.scalar.copy(out=dst, in_=src)
+            grps[key] = grp
+
+        def quant(key):
+            i = int(key[1:])
+            grp = grps[key]
             if key[0] == "d":
                 nc.vector.quantize_mx(out=dc[i][:].bitcast(FP8X4), scales=ds[i][:], in_=grp[:])
             else:
@@ -126,11 +132,15 @@ def tile_linear_pa_kernel(tc, data, W, t_lora, lora_b, out_0, out_1):
                         in_=grp[:, 512 * g : 512 * (g + 1)],
                     )
 
+        def xpose(key):
+            x_t(key)
+            quant(key)
+
         def xpose_tl():
             bank = psum.tile([P, 1024], BF16, tag="bank", name="tlT")
             for a in range(B):
                 nc.tensor.transpose(bank[:, S * a : S * (a + 1)], tl[:, a, :], ident_b[:])
-            nc.vector.tensor_copy(out=tT[:].rearrange("p a s -> p (a s)"), in_=bank[:])
+            nc.scalar.copy(out=tT[:].rearrange("p a s -> p (a s)"), in_=bank[:])
 
         def xpose_lb(l):
             bank = psum.tile([P, 1024], BF16, tag="bank", name="lbx%d" % l)
@@ -157,34 +167,42 @@ def tile_linear_pa_kernel(tc, data, W, t_lora, lora_b, out_0, out_1):
                 )
                 lsb[(b, n)] = t_sb
 
-        def mx_mm(s):
+        def mx(s, e):
             n = s // 4
-            for e in range(2):
-                b = 2 * (s % 4) + e
-                acc = psum.tile([P, NT], F32, tag="bank", name="acc%d_%d" % (b, n))
+            b = 2 * (s % 4) + e
+            last = s == SLOTS - 1 and e == 1
+            width = NT // 2 if last else NT
+            for c0 in range(0, NT, width):
+                acc = psum.tile([P, width], F32, tag="bank", name="acc%d_%d_%d" % (b, n, c0))
                 for g in range(PASSES):
                     nc.tensor.matmul_mx(
                         out=acc[:],
                         lhsT=dc[b][:, P * g : P * (g + 1)].bitcast(FP8X4),
                         lhsT_scale=ds[b][:, P * g : P * (g + 1)],
-                        rhs=wc[n][:, g, :].bitcast(FP8X4),
-                        rhs_scale=ws[n][:, g, :],
+                        rhs=wc[n][:, g, c0 : c0 + width].bitcast(FP8X4),
+                        rhs_scale=ws[n][:, g, c0 : c0 + width],
                         start=(g == 0),
                         stop=(g == PASSES - 1),
                     )
-                o0 = o0p.tile([P, NT], F32, tag="o0", name="o0_%d_%d" % (b, n))
-                nc.vector.tensor_tensor(out=o0[:], in0=acc[:], in1=lsb[(b, n)][:], op=ALU.add)
-                nc.sync.dma_start(out=out_0[b, :, NT * n : NT * (n + 1)], in_=o0[:])
-                nc.vector.tensor_scalar(
-                    out=o1[b][:, NT * n : NT * (n + 1)],
-                    in0=o0[:],
-                    scalar1=150.0,
-                    scalar2=None,
-                    op0=ALU.mult,
-                    saturate=False,
-                )
+                o0 = o0p.tile([P, width], F32, tag="o0", name="o0_%d_%d_%d" % (b, n, c0))
+                nc.vector.tensor_tensor(out=o0[:], in0=acc[:], in1=lsb[(b, n)][:, c0 : c0 + width], op=ALU.add)
+                lo = NT * n + c0
+                nc.sync.dma_start(out=out_0[b, :, lo : lo + width], in_=o0[:])
+                if s == SLOTS - 1:
+                    nc.scalar.activation(out=o1[b][:, lo : lo + width], in_=o0[:], func=ACT.Copy, scale=150.0, saturate=False)
+                else:
+                    nc.vector.tensor_scalar(
+                        out=o1[b][:, lo : lo + width],
+                        in0=o0[:],
+                        scalar1=150.0,
+                        scalar2=None,
+                        op0=ALU.mult,
+                        saturate=False,
+                    )
+                if n == 2:
+                    nc.sync.dma_start(out=out_1[b, :, 0 : 3 * NT], in_=o1[b][:, 0 : 3 * NT].bitcast(U8))
                 if n == 3:
-                    nc.sync.dma_start(out=out_1[b], in_=o1[b][:].bitcast(U8))
+                    nc.sync.dma_start(out=out_1[b, :, lo : lo + width], in_=o1[b][:, lo : lo + width].bitcast(U8))
 
         def slot_tiles(s):
             keys = []
@@ -221,17 +239,39 @@ def tile_linear_pa_kernel(tc, data, W, t_lora, lora_b, out_0, out_1):
         xpose("d1")
         lora_mm(0)
 
-        for s in range(SLOTS):
-            slot_loads(s + LA)
-            keys = slot_tiles(s)
-            for key in slot_tiles(s + 1):
-                precopy(key)
-            for key in keys[:-1]:
-                xpose(key)
-            if s + 1 < SLOTS:
-                xpose_lb(s + 1)
-            for key in keys[-1:]:
-                xpose(key)
-            mx_mm(s)
-            if s + 1 < SLOTS:
-                lora_mm(s + 1)
+        for gi in range(len(GROUPS)):
+            group = GROUPS[gi]
+            later = GROUPS[gi + 1] if gi + 1 < len(GROUPS) else ()
+            for s in group:
+                slot_loads(s + LA)
+            for s in later:
+                for key in slot_tiles(s):
+                    precopy(key)
+            for s in group:
+                for key in slot_tiles(s)[:-1]:
+                    xpose(key)
+            for s in later:
+                xpose_lb(s)
+            w_keys = []
+            for s in group:
+                w_keys.extend(slot_tiles(s)[-1:])
+            for key in w_keys:
+                x_t(key)
+            if len(group) == 1:
+                for key in w_keys:
+                    quant(key)
+                mx(group[0], 0)
+                mx(group[0], 1)
+                for s in later:
+                    lora_mm(s)
+            else:
+                for key in w_keys[:1]:
+                    quant(key)
+                mx(group[0], 0)
+                for key in w_keys[1:]:
+                    quant(key)
+                mx(group[0], 1)
+                for s in later:
+                    lora_mm(s)
+                mx(group[1], 0)
+                mx(group[1], 1)

@@ -22,6 +22,7 @@ SLOTS = 16
 
 RAW_BUFS = 14
 GROUPS = ((0,), (1,), (2,), (3,), (4, 5), (6, 7), (8, 9), (10, 11), (12, 13), (14, 15))
+CAST_LAG = 1
 LA = 5
 PRECOPY = ("w7", "w8", "w9", "w10", "w11", "w12", "w13", "w14", "w15")
 V_EVAC = ("d0", "d1", "d2", "d3", "d4", "d5", "d6", "d7", "w0", "w1", "w2", "w3")
@@ -63,6 +64,7 @@ def tile_linear_pa_kernel(tc, data, W, t_lora, lora_b, out_0, out_1):
         lbT = {}
         lsb = {}
         grps = {}
+        waiting = []
 
         def load(key):
             i = int(key[1:])
@@ -188,21 +190,28 @@ def tile_linear_pa_kernel(tc, data, W, t_lora, lora_b, out_0, out_1):
                 nc.vector.tensor_tensor(out=o0[:], in0=acc[:], in1=lsb[(b, n)][:, c0 : c0 + width], op=ALU.add)
                 lo = NT * n + c0
                 nc.sync.dma_start(out=out_0[b, :, lo : lo + width], in_=o0[:])
-                if s == SLOTS - 1:
-                    nc.scalar.activation(out=o1[b][:, lo : lo + width], in_=o0[:], func=ACT.Copy, scale=150.0, saturate=False)
-                else:
-                    nc.vector.tensor_scalar(
-                        out=o1[b][:, lo : lo + width],
-                        in0=o0[:],
-                        scalar1=150.0,
-                        scalar2=None,
-                        op0=ALU.mult,
-                        saturate=False,
-                    )
-                if n == 2:
-                    nc.sync.dma_start(out=out_1[b, :, 0 : 3 * NT], in_=o1[b][:, 0 : 3 * NT].bitcast(U8))
-                if n == 3:
-                    nc.sync.dma_start(out=out_1[b, :, lo : lo + width], in_=o1[b][:, lo : lo + width].bitcast(U8))
+                waiting.append((s, b, n, lo, width, o0))
+                lag = 0 if s == SLOTS - 1 else CAST_LAG
+                for item in waiting[: max(0, len(waiting) - lag)]:
+                    cast(*item)
+                    waiting.remove(item)
+
+        def cast(s, b, n, lo, width, o0):
+            if s == SLOTS - 1 or (s >= 4 and b % 4 == 4 - 1):
+                nc.scalar.activation(out=o1[b][:, lo : lo + width], in_=o0[:], func=ACT.Copy, scale=150.0, saturate=False)
+            else:
+                nc.vector.tensor_scalar(
+                    out=o1[b][:, lo : lo + width],
+                    in0=o0[:],
+                    scalar1=150.0,
+                    scalar2=None,
+                    op0=ALU.mult,
+                    saturate=False,
+                )
+            if n == 2:
+                nc.sync.dma_start(out=out_1[b, :, 0 : 3 * NT], in_=o1[b][:, 0 : 3 * NT].bitcast(U8))
+            if n == 3:
+                nc.sync.dma_start(out=out_1[b, :, lo : lo + width], in_=o1[b][:, lo : lo + width].bitcast(U8))
 
         def slot_tiles(s):
             keys = []
@@ -271,7 +280,7 @@ def tile_linear_pa_kernel(tc, data, W, t_lora, lora_b, out_0, out_1):
                 for key in w_keys[1:]:
                     quant(key)
                 mx(group[0], 1)
-                for s in later:
-                    lora_mm(s)
                 mx(group[1], 0)
                 mx(group[1], 1)
+                for s in later:
+                    lora_mm(s)

@@ -20,11 +20,18 @@ NT = 512
 PASSES = IN // 512
 SLOTS = 16
 
-RAW_BUFS = 14
+RAW_BUFS = 8
+HALF_BUFS = 12
 GROUPS = ((0,), (1,), (2,), (3,), (4, 5), (6, 7), (8, 9), (10, 11), (12, 13), (14, 15))
 CAST_LAG = 1
 LA = 5
-PRECOPY = ("w7", "w8", "w9", "w10", "w11", "w12", "w13", "w14", "w15")
+PRECOPY = ("d4", "d5", "d6", "d7", "w6", "w7", "w8", "w9", "w10", "w11", "w12", "w13", "w14", "w15")
+SPLIT = ("d0", "d1", "d2", "d3", "w0", "w1", "w2", "w3", "w4", "w5")
+S_PRECOPY = {"d4": 0, "d6": 1, "w6": 1}
+HEAD_LORA_LATE = False
+V_PC_MID = {"d5": 0, "d7": 1}
+V_PC_START = {}
+V_PC_END = {}
 V_EVAC = ("d0", "d1", "d2", "d3", "d4", "d5", "d6", "d7", "w0", "w1", "w2", "w3")
 
 
@@ -33,6 +40,7 @@ def tile_linear_pa_kernel(tc, data, W, t_lora, lora_b, out_0, out_1):
     with ExitStack() as ctx:
         const = ctx.enter_context(tc.tile_pool(name="const", bufs=1))
         rawp = ctx.enter_context(tc.tile_pool(name="rawp", bufs=RAW_BUFS))
+        rawhp = ctx.enter_context(tc.tile_pool(name="rawhp", bufs=HALF_BUFS))
         pcp = ctx.enter_context(tc.tile_pool(name="pcp", bufs=4))
         grpp = ctx.enter_context(tc.tile_pool(name="grpp", bufs=4))
         codes = ctx.enter_context(tc.tile_pool(name="codes", bufs=1))
@@ -65,15 +73,22 @@ def tile_linear_pa_kernel(tc, data, W, t_lora, lora_b, out_0, out_1):
         lsb = {}
         grps = {}
         waiting = []
+        accs = {}
 
         def load(key):
             i = int(key[1:])
-            t = rawp.tile([P, IN], BF16, tag="raw", name="raw_" + key)
-            if key[0] == "d":
-                nc.sync.dma_start(out=t[:], in_=data[i])
+            rows = data[i] if key[0] == "d" else W[P * i : P * (i + 1), :]
+            if key in SPLIT:
+                halves = []
+                for h in range(2):
+                    t = rawhp.tile([P, IN // 2], BF16, tag="rawh", name="raw_%s_%d" % (key, h))
+                    nc.sync.dma_start(out=t[:], in_=rows[:, (IN // 2) * h : (IN // 2) * (h + 1)])
+                    halves.append(t)
+                raw[key] = halves
             else:
-                nc.sync.dma_start(out=t[:], in_=W[P * i : P * (i + 1), :])
-            raw[key] = t
+                t = rawp.tile([P, IN], BF16, tag="raw", name="raw_" + key)
+                nc.sync.dma_start(out=t[:], in_=rows)
+                raw[key] = t
 
         def load_lb(l):
             n, a2 = l // 4, l % 4
@@ -84,8 +99,8 @@ def tile_linear_pa_kernel(tc, data, W, t_lora, lora_b, out_0, out_1):
             )
             lbraw[l] = t
 
-        def precopy(key):
-            if key not in PRECOPY:
+        def precopy(key, forced=False):
+            if key not in PRECOPY or key in S_PRECOPY or ((key in V_PC_MID or key in V_PC_END or key in V_PC_START) and not forced):
                 return
             pc = pcp.tile([P, IN // 2], F32, tag="pc", name="pc_" + key)
             nc.vector.tensor_copy(
@@ -94,11 +109,17 @@ def tile_linear_pa_kernel(tc, data, W, t_lora, lora_b, out_0, out_1):
             )
             raw[key] = pc
 
+        def precopy_s(key):
+            pc = pcp.tile([P, IN // 2], F32, tag="pc", name="pc_" + key)
+            nc.scalar.copy(
+                out=pc[:].rearrange("p (g u w) -> p g u w", g=PASSES, u=2),
+                in_=raw[key][:].bitcast(F32).rearrange("p (g w u) -> p g u w", g=PASSES, u=2),
+            )
+            raw[key] = pc
+
         def x_t(key):
             if key in PRECOPY:
                 words = raw[key][:]
-            else:
-                words = raw[key][:].bitcast(F32)
             grp = grpp.tile([P, IN], BF16, tag="grp", name="grp_" + key, align_bytes=64)
             grp_w = grp[:].bitcast(F32)
             for h in range(2):
@@ -109,7 +130,7 @@ def tile_linear_pa_kernel(tc, data, W, t_lora, lora_b, out_0, out_1):
                         if key in PRECOPY:
                             src = words[:, 256 * g + 128 * u : 256 * g + 128 * (u + 1)]
                         else:
-                            src = words[:, 256 * g + u : 256 * (g + 1) : 2]
+                            src = raw[key][h][:].bitcast(F32)[:, 256 * g2 + u : 256 * (g2 + 1) : 2]
                         c = 128 * (2 * g2 + u)
                         nc.tensor.transpose(bank[:, c : c + 128], src, ident_f[:])
                 src = bank[:].rearrange("p (g u r) -> p g r u", g=2, u=2)
@@ -170,12 +191,18 @@ def tile_linear_pa_kernel(tc, data, W, t_lora, lora_b, out_0, out_1):
                 lsb[(b, n)] = t_sb
 
         def mx(s, e):
-            n = s // 4
-            b = 2 * (s % 4) + e
             last = s == SLOTS - 1 and e == 1
             width = NT // 2 if last else NT
             for c0 in range(0, NT, width):
+                mx_pe(s, e, c0, width)
+                mx_out(s, e, c0, width)
+
+        def mx_pe(s, e, c0, width):
+            n = s // 4
+            b = 2 * (s % 4) + e
+            if True:
                 acc = psum.tile([P, width], F32, tag="bank", name="acc%d_%d_%d" % (b, n, c0))
+                accs[(b, n, c0)] = acc
                 for g in range(PASSES):
                     nc.tensor.matmul_mx(
                         out=acc[:],
@@ -186,6 +213,12 @@ def tile_linear_pa_kernel(tc, data, W, t_lora, lora_b, out_0, out_1):
                         start=(g == 0),
                         stop=(g == PASSES - 1),
                     )
+
+        def mx_out(s, e, c0, width):
+            n = s // 4
+            b = 2 * (s % 4) + e
+            if True:
+                acc = accs[(b, n, c0)]
                 o0 = o0p.tile([P, width], F32, tag="o0", name="o0_%d_%d_%d" % (b, n, c0))
                 nc.vector.tensor_tensor(out=o0[:], in0=acc[:], in1=lsb[(b, n)][:, c0 : c0 + width], op=ALU.add)
                 lo = NT * n + c0
@@ -239,26 +272,38 @@ def tile_linear_pa_kernel(tc, data, W, t_lora, lora_b, out_0, out_1):
         load("d1")
         for s in range(LA):
             slot_loads(s)
-        for key in ("d0", "w0", "w1", "w2", "w3"):
-            precopy(key)
+        x_t("d0")
+        x_t("w0")
+        quant("d0")
+        quant("w0")
+        for key in ("w1", "w2", "w3"):
             xpose(key)
         xpose_tl()
         xpose_lb(0)
-        precopy("d1")
-        xpose("d1")
-        lora_mm(0)
+        x_t("d1")
+        pending = ["d1"]
+        if not HEAD_LORA_LATE:
+            lora_mm(0)
 
         for gi in range(len(GROUPS)):
             group = GROUPS[gi]
             later = GROUPS[gi + 1] if gi + 1 < len(GROUPS) else ()
             for s in group:
                 slot_loads(s + LA)
+            for key in sorted(V_PC_START):
+                if V_PC_START[key] == group[0]:
+                    precopy(key, True)
             for s in later:
                 for key in slot_tiles(s):
                     precopy(key)
+            d_keys = []
             for s in group:
-                for key in slot_tiles(s)[:-1]:
-                    xpose(key)
+                d_keys.extend(slot_tiles(s)[:-1])
+            for key in d_keys:
+                x_t(key)
+            for key in pending + d_keys:
+                quant(key)
+            pending.clear()
             for s in later:
                 xpose_lb(s)
             w_keys = []
@@ -266,21 +311,34 @@ def tile_linear_pa_kernel(tc, data, W, t_lora, lora_b, out_0, out_1):
                 w_keys.extend(slot_tiles(s)[-1:])
             for key in w_keys:
                 x_t(key)
-            if len(group) == 1:
+            for key in sorted(S_PRECOPY):
+                if S_PRECOPY[key] == group[0]:
+                    precopy_s(key)
+            tiles = [(s, e) for s in group for e in range(2)]
+            if gi == 0 and HEAD_LORA_LATE:
                 for key in w_keys:
                     quant(key)
-                mx(group[0], 0)
-                mx(group[0], 1)
+                for (s, e) in tiles:
+                    mx_pe(s, e, 0, NT)
+                lora_mm(0)
                 for s in later:
                     lora_mm(s)
+                for (s, e) in tiles:
+                    mx_out(s, e, 0, NT)
             else:
-                for key in w_keys[:1]:
-                    quant(key)
-                mx(group[0], 0)
-                for key in w_keys[1:]:
-                    quant(key)
-                mx(group[0], 1)
-                mx(group[1], 0)
-                mx(group[1], 1)
+                if len(group) == 1:
+                    for key in w_keys:
+                        quant(key)
+                for key in sorted(V_PC_MID):
+                    if V_PC_MID[key] == group[0]:
+                        precopy(key, True)
+                for i in range(len(tiles)):
+                    if len(group) > 1 and i < len(w_keys):
+                        quant(w_keys[i])
+                    mx(tiles[i][0], tiles[i][1])
+                    if i == 0:
+                        for key in sorted(V_PC_END):
+                            if V_PC_END[key] == group[0]:
+                                precopy(key, True)
                 for s in later:
                     lora_mm(s)

@@ -20,13 +20,13 @@ NT = 512
 PASSES = IN // 512
 SLOTS = 16
 
-RAW_BUFS = 8
-HALF_BUFS = 12
+RAW_BUFS = 14
+HALF_BUFS = 1
 GROUPS = ((0,), (1,), (2,), (3,), (4, 5), (6, 7), (8, 9), (10, 11), (12, 13), (14, 15))
 CAST_LAG = 1
 LA = 5
 PRECOPY = ("d4", "d5", "d6", "d7", "w6", "w7", "w8", "w9", "w10", "w11", "w12", "w13", "w14", "w15")
-SPLIT = ("d0", "d1", "d2", "d3", "w0", "w1", "w2", "w3", "w4", "w5")
+SPLIT = ()
 S_PRECOPY = {"d4": 0, "d6": 1, "w6": 1}
 HEAD_LORA_LATE = False
 V_PC_MID = {"d5": 0, "d7": 1}
@@ -129,8 +129,10 @@ def tile_linear_pa_kernel(tc, data, W, t_lora, lora_b, out_0, out_1):
                     for u in range(2):
                         if key in PRECOPY:
                             src = words[:, 256 * g + 128 * u : 256 * g + 128 * (u + 1)]
-                        else:
+                        elif key in SPLIT:
                             src = raw[key][h][:].bitcast(F32)[:, 256 * g2 + u : 256 * (g2 + 1) : 2]
+                        else:
+                            src = raw[key][:].bitcast(F32)[:, 256 * g + u : 256 * (g + 1) : 2]
                         c = 128 * (2 * g2 + u)
                         nc.tensor.transpose(bank[:, c : c + 128], src, ident_f[:])
                 src = bank[:].rearrange("p (g u r) -> p g r u", g=2, u=2)

@@ -25,12 +25,12 @@ HALF_BUFS = 1
 GROUPS = ((0,), (1,), (2,), (3,), (4, 5), (6, 7), (8, 9), (10, 11), (12, 13), (14, 15))
 CAST_LAG = 1
 LA = 5
-PRECOPY = ("d4", "d5", "d6", "d7", "w6", "w7", "w8", "w9", "w10", "w11", "w12", "w13", "w14", "w15")
+PRECOPY = ("d6", "d7", "w6", "w7", "w8", "w9", "w10", "w11", "w12", "w13", "w14", "w15")
 SPLIT = ()
-S_PRECOPY = {"d4": 0, "d6": 1, "w6": 1}
+S_PRECOPY = {"d6": 1, "d7": 1, "w7": 2, "w8": 3}
 HEAD_LORA_LATE = False
-V_PC_MID = {"d5": 0, "d7": 1}
-V_PC_START = {}
+V_PC_MID = {"w9": 3}
+V_PC_START = {"w6": 2}
 V_PC_END = {}
 V_EVAC = ("d0", "d1", "d2", "d3", "d4", "d5", "d6", "d7", "w0", "w1", "w2", "w3")
 
@@ -49,7 +49,7 @@ def tile_linear_pa_kernel(tc, data, W, t_lora, lora_b, out_0, out_1):
         lsbp = ctx.enter_context(tc.tile_pool(name="lsbp", bufs=10))
         o0p = ctx.enter_context(tc.tile_pool(name="o0p", bufs=6))
         psum = ctx.enter_context(tc.psum_pool(name="psum", bufs=8))
-        ctx.enter_context(tc.manual_schedule(engines={mybir.EngineType.PE, mybir.EngineType.DVE, mybir.EngineType.Activation}))
+        ctx.enter_context(tc.manual_schedule(engines={mybir.EngineType.PE, mybir.EngineType.DVE, mybir.EngineType.Activation, mybir.EngineType.SP}))
 
         ident_f = const.tile([P, P], F32, name="ident_f")
         make_identity(nc, ident_f[:])
@@ -163,9 +163,12 @@ def tile_linear_pa_kernel(tc, data, W, t_lora, lora_b, out_0, out_1):
 
         def xpose_tl():
             bank = psum.tile([P, 1024], BF16, tag="bank", name="tlT")
-            for a in range(B):
-                nc.tensor.transpose(bank[:, S * a : S * (a + 1)], tl[:, a, :], ident_b[:])
-            nc.scalar.copy(out=tT[:].rearrange("p a s -> p (a s)"), in_=bank[:])
+            for j in range(B):
+                nc.tensor.transpose(bank[:, S * j : S * (j + 1)], tl[:, j, :], ident_b[:])
+            nc.scalar.copy(
+                out=tT[:].rearrange("p m (q j) -> p m q j", j=B),
+                in_=bank[:].rearrange("p (j m q) -> p m q j", j=B, m=B),
+            )
 
         def xpose_lb(l):
             bank = psum.tile([P, 1024], BF16, tag="bank", name="lbx%d" % l)
@@ -269,7 +272,7 @@ def tile_linear_pa_kernel(tc, data, W, t_lora, lora_b, out_0, out_1):
 
         for key in ("d0", "w0", "w1", "w2", "w3"):
             load(key)
-        nc.sync.dma_start(out=tl[:], in_=t_lora.rearrange("a g s r -> s (a g) r"))
+        nc.sync.dma_start(out=tl[:], in_=t_lora.rearrange("a g (q j) r -> (a g q) j r", j=B))
         load_lb(0)
         load("d1")
         for s in range(LA):

from contextlib import ExitStack

import concourse.mybir as mybir
from concourse.masks import make_identity

B, S, IN, OUT, R = 8, 128, 2048, 2048, 128
FLOPS = 2 * B * S * OUT * IN + 2 * B * S * OUT * R

F32 = mybir.dt.float32
BF16 = mybir.dt.bfloat16
U32 = mybir.dt.uint32
U8 = mybir.dt.uint8
FP8X4 = mybir.dt.float8_e4m3fn_x4
FP8 = mybir.dt.float8_e4m3fn
ACT = mybir.ActivationFunctionType
ALU = mybir.AluOpType

P = 128
NT = 512
PASSES = IN // 512
SLOTS = 16

RAW_BUFS = 14
HALF_BUFS = 1
GROUPS = ((0,), (1,), (2,), (3,), (4, 5), (6, 7), (8, 9), (10, 11), (12, 13), (14, 15))
CAST_LAG = 1
LA = 5
PRECOPY = ("d6", "d7", "w6", "w7", "w8", "w9", "w10", "w11", "w12", "w13", "w14", "w15")
SPLIT = ()
S_PRECOPY = {"d6": 1, "d7": 1, "w7": 2, "w8": 3}
HEAD_LORA_LATE = False
V_PC_MID = {"w9": 3}
V_PC_START = {"w6": 2}
V_PC_END = {}
V_EVAC = ("d0", "d1", "d2", "d3", "d4", "d5", "d6", "d7", "w0", "w1", "w2", "w3")


def tile_linear_pa_kernel(tc, data, W, t_lora, lora_b, out_0, out_1):
    nc = tc.nc
    with ExitStack() as ctx:
        const = ctx.enter_context(tc.tile_pool(name="const", bufs=1))
        rawp = ctx.enter_context(tc.tile_pool(name="rawp", bufs=RAW_BUFS))
        rawhp = ctx.enter_context(tc.tile_pool(name="rawhp", bufs=HALF_BUFS))
        pcp = ctx.enter_context(tc.tile_pool(name="pcp", bufs=4))
        grpp = ctx.enter_context(tc.tile_pool(name="grpp", bufs=4))
        codes = ctx.enter_context(tc.tile_pool(name="codes", bufs=1))
        lbrp = ctx.enter_context(tc.tile_pool(name="lbrp", bufs=8))
        lbtp = ctx.enter_context(tc.tile_pool(name="lbtp", bufs=4))
        lsbp = ctx.enter_context(tc.tile_pool(name="lsbp", bufs=10))
        o0p = ctx.enter_context(tc.tile_pool(name="o0p", bufs=6))
        psum = ctx.enter_context(tc.psum_pool(name="psum", bufs=8))
        ctx.enter_context(tc.manual_schedule(engines={mybir.EngineType.PE, mybir.EngineType.DVE, mybir.EngineType.Activation, mybir.EngineType.SP}))

        ident_f = const.tile([P, P], F32, name="ident_f")
        make_identity(nc, ident_f[:])
        ident_b = const.tile([P, P], BF16, name="ident_b")
        make_identity(nc, ident_b[:])
        warm = const.tile([P, 2], F32, name="warm")
        nc.vector.memset(warm[:], 0.0)
        nc.scalar.activation(out=warm[:, 1:2], in_=warm[:, 0:1], func=ACT.Copy, scale=2.0)

        tl = const.tile([P, B, R], BF16, name="tl")
        tT = const.tile([P, B, S], BF16, name="tT")
        dc = [codes.tile([P, 512], U32, name="dc%d" % b, align_bytes=64) for b in range(B)]
        ds = [codes.tile([P, 512], U8, name="ds%d" % b, align_bytes=64) for b in range(B)]
        wc = [codes.tile([P, PASSES, NT], U32, name="wc%d" % n, align_bytes=64) for n in range(4)]
        ws = [codes.tile([P, PASSES, NT], U8, name="ws%d" % n, align_bytes=64) for n in range(4)]
        o1 = [codes.tile([P, OUT], FP8, name="o1_%d" % b) for b in range(B)]

        raw = {}
        lbraw = {}
        lbT = {}
        lsb = {}
        grps = {}
        waiting = []
        accs = {}

        def load(key):
            i = int(key[1:])
            rows = data[i] if key[0] == "d" else W[P * i : P * (i + 1), :]
            if key in SPLIT:
                halves = []
                for h in range(2):
                    t = rawhp.tile([P, IN // 2], BF16, tag="rawh", name="raw_%s_%d" % (key, h))
                    nc.sync.dma_start(out=t[:], in_=rows[:, (IN // 2) * h : (IN // 2) * (h + 1)])
                    halves.append(t)
                raw[key] = halves
            else:
                t = rawp.tile([P, IN], BF16, tag="raw", name="raw_" + key)
                nc.sync.dma_start(out=t[:], in_=rows)
                raw[key] = t

        def load_lb(l):
            n, a2 = l // 4, l % 4
            t = lbrp.tile([P, 2, NT], BF16, tag="lbraw", name="lbraw%d" % l)
            nc.sync.dma_start(
                out=t[:],
                in_=lora_b[2 * a2 : 2 * a2 + 2, NT * n : NT * (n + 1), :].rearrange("a (p t) r -> p a (t r)", t=4),
            )
            lbraw[l] = t

        def precopy(key, forced=False):
            if key not in PRECOPY or key in S_PRECOPY or ((key in V_PC_MID or key in V_PC_END or key in V_PC_START) and not forced):
                return
            pc = pcp.tile([P, IN // 2], F32, tag="pc", name="pc_" + key)
            nc.vector.tensor_copy(
                out=pc[:].rearrange("p (g u w) -> p g u w", g=PASSES, u=2),
                in_=raw[key][:].bitcast(F32).rearrange("p (g w u) -> p g u w", g=PASSES, u=2),
            )
            raw[key] = pc

        def precopy_s(key):
            pc = pcp.tile([P, IN // 2], F32, tag="pc", name="pc_" + key)
            nc.scalar.copy(
                out=pc[:].rearrange("p (g u w) -> p g u w", g=PASSES, u=2),
                in_=raw[key][:].bitcast(F32).rearrange("p (g w u) -> p g u w", g=PASSES, u=2),
            )
            raw[key] = pc

        def x_t(key):
            if key in PRECOPY:
                words = raw[key][:]
            grp = grpp.tile([P, IN], BF16, tag="grp", name="grp_" + key, align_bytes=64)
            grp_w = grp[:].bitcast(F32)
            for h in range(2):
                bank = psum.tile([P, 512], F32, tag="bank", name="xt_%s_%d" % (key, h))
                for g2 in range(2):
                    g = 2 * h + g2
                    for u in range(2):
                        if key in PRECOPY:
                            src = words[:, 256 * g + 128 * u : 256 * g + 128 * (u + 1)]
                        elif key in SPLIT:
                            src = raw[key][h][:].bitcast(F32)[:, 256 * g2 + u : 256 * (g2 + 1) : 2]
                        else:
                            src = raw[key][:].bitcast(F32)[:, 256 * g + u : 256 * (g + 1) : 2]
                        c = 128 * (2 * g2 + u)
                        nc.tensor.transpose(bank[:, c : c + 128], src, ident_f[:])
                src = bank[:].rearrange("p (g u r) -> p g r u", g=2, u=2)
                dst = grp_w[:, 512 * h : 512 * (h + 1)].rearrange("p (g r u) -> p g r u", g=2, u=2)
                if h == 1 and key in V_EVAC:
                    nc.vector.tensor_copy(out=dst, in_=src)
                else:
                    nc.scalar.copy(out=dst, in_=src)
            grps[key] = grp

        def quant(key):
            i = int(key[1:])
            grp = grps[key]
            if key[0] == "d":
                nc.vector.quantize_mx(out=dc[i][:].bitcast(FP8X4), scales=ds[i][:], in_=grp[:])
            else:
                n, j = i // 4, i % 4
                for g in range(PASSES):
                    nc.vector.quantize_mx(
                        out=wc[n][:, g, P * j : P * (j + 1)].bitcast(FP8X4),
                        scales=ws[n][:, g, P * j : P * (j + 1)],
                        in_=grp[:, 512 * g : 512 * (g + 1)],
                    )

        def xpose(key):
            x_t(key)
            quant(key)

        def xpose_tl():
            bank = psum.tile([P, 1024], BF16, tag="bank", name="tlT")
            for j in range(B):
                nc.tensor.transpose(bank[:, S * j : S * (j + 1)], tl[:, j, :], ident_b[:])
            nc.scalar.copy(
                out=tT[:].rearrange("p m (q j) -> p m q j", j=B),
                in_=bank[:].rearrange("p (j m q) -> p m q j", j=B, m=B),
            )

        def xpose_lb(l):
            bank = psum.tile([P, 1024], BF16, tag="bank", name="lbx%d" % l)
            for a in range(2):
                for t in range(4):
                    c = 512 * a + 128 * t
                    nc.tensor.transpose(bank[:, c : c + 128], lbraw[l][:, a, 128 * t : 128 * (t + 1)], ident_b[:])
            t_sb = lbtp.tile([P, 2, NT], BF16, tag="lbT", name="lbT%d" % l)
            nc.scalar.copy(out=t_sb[:].rearrange("p a c -> p (a c)"), in_=bank[:])
            lbT[l] = t_sb

        def lora_mm(s):
            n = s // 4
            for e in range(2):
                b = 2 * (s % 4) + e
                lp = psum.tile([P, NT], F32, tag="bank", name="lp%d_%d" % (b, n))
                nc.tensor.matmul(lp[:], lhsT=tT[:, b, :], rhs=lbT[s][:, e, :], start=True, stop=True)
                t_sb = lsbp.tile([P, NT], F32, tag="lsb", name="lsb%d_%d" % (b, n))
                nc.scalar.activation(
                    out=t_sb[:].rearrange("s (p t) -> s p t", t=4),
                    in_=lp[:].rearrange("s (t p) -> s p t", t=4),
                    func=ACT.Copy,
                    scale=2.0,
                )
                lsb[(b, n)] = t_sb

        def mx(s, e):
            last = s == SLOTS - 1 and e == 1
            width = NT // 2 if last else NT
            for c0 in range(0, NT, width):
                mx_pe(s, e, c0, width)
                mx_out(s, e, c0, width)

        def mx_pe(s, e, c0, width):
            n = s // 4
            b = 2 * (s % 4) + e
            if True:
                acc = psum.tile([P, width], F32, tag="bank", name="acc%d_%d_%d" % (b, n, c0))
                accs[(b, n, c0)] = acc
                for g in range(PASSES):
                    nc.tensor.matmul_mx(
                        out=acc[:],
                        lhsT=dc[b][:, P * g : P * (g + 1)].bitcast(FP8X4),
                        lhsT_scale=ds[b][:, P * g : P * (g + 1)],
                        rhs=wc[n][:, g, c0 : c0 + width].bitcast(FP8X4),
                        rhs_scale=ws[n][:, g, c0 : c0 + width],
                        start=(g == 0),
                        stop=(g == PASSES - 1),
                    )

        def mx_out(s, e, c0, width):
            n = s // 4
            b = 2 * (s % 4) + e
            if True:
                acc = accs[(b, n, c0)]
                o0 = o0p.tile([P, width], F32, tag="o0", name="o0_%d_%d_%d" % (b, n, c0))
                nc.vector.tensor_tensor(out=o0[:], in0=acc[:], in1=lsb[(b, n)][:, c0 : c0 + width], op=ALU.add)
                lo = NT * n + c0
                nc.sync.dma_start(out=out_0[b, :, lo : lo + width], in_=o0[:])
                waiting.append((s, b, n, lo, width, o0))
                lag = 0 if s == SLOTS - 1 else CAST_LAG
                for item in waiting[: max(0, len(waiting) - lag)]:
                    cast(*item)
                    waiting.remove(item)

        def cast(s, b, n, lo, width, o0):
            if s == SLOTS - 1 or (s >= 4 and b % 4 == 4 - 1):
                nc.scalar.activation(out=o1[b][:, lo : lo + width], in_=o0[:], func=ACT.Copy, scale=150.0, saturate=False)
            else:
                nc.vector.tensor_scalar(
                    out=o1[b][:, lo : lo + width],
                    in0=o0[:],
                    scalar1=150.0,
                    scalar2=None,
                    op0=ALU.mult,
                    saturate=False,
                )
            if n == 2:
                nc.sync.dma_start(out=out_1[b, :, 0 : 3 * NT], in_=o1[b][:, 0 : 3 * NT].bitcast(U8))
            if n == 3:
                nc.sync.dma_start(out=out_1[b, :, lo : lo + width], in_=o1[b][:, lo : lo + width].bitcast(U8))

        def slot_tiles(s):
            keys = []
            if s <= 2:
                keys = ["d%d" % (2 * s + 2), "d%d" % (2 * s + 3)]
            if s <= 11:
                keys.append("w%d" % (4 + s))
            return keys

        def slot_loads(s):
            if s >= SLOTS:
                return
            keys = slot_tiles(s)
            for key in keys[:-1]:
                load(key)
            if s + 1 < SLOTS:
                load_lb(s + 1)
            for key in keys[-1:]:
                load(key)

        for key in ("d0", "w0", "w1", "w2", "w3"):
            load(key)
        nc.sync.dma_start(out=tl[:], in_=t_lora.rearrange("a g (q j) r -> (a g q) j r", j=B))
        load_lb(0)
        load("d1")
        for s in range(LA):
            slot_loads(s)
        x_t("d0")
        x_t("w0")
        quant("d0")
        quant("w0")
        for key in ("w1", "w2", "w3"):
            xpose(key)
        xpose_tl()
        xpose_lb(0)
        x_t("d1")
        pending = ["d1"]
        if not HEAD_LORA_LATE:
            lora_mm(0)

        for gi in range(len(GROUPS)):
            group = GROUPS[gi]
            later = GROUPS[gi + 1] if gi + 1 < len(GROUPS) else ()
            for s in group:
                slot_loads(s + LA)
            for key in sorted(V_PC_START):
                if V_PC_START[key] == group[0]:
                    precopy(key, True)
            for s in later:
                for key in slot_tiles(s):
                    precopy(key)
            d_keys = []
            for s in group:
                d_keys.extend(slot_tiles(s)[:-1])
            for key in d_keys:
                x_t(key)
            for key in pending + d_keys:
                quant(key)
            pending.clear()
            for s in later:
                xpose_lb(s)
            w_keys = []
            for s in group:
                w_keys.extend(slot_tiles(s)[-1:])
            for key in w_keys:
                x_t(key)
            for key in sorted(S_PRECOPY):
                if S_PRECOPY[key] == group[0]:
                    precopy_s(key)
            tiles = [(s, e) for s in group for e in range(2)]
            if gi == 0 and HEAD_LORA_LATE:
                for key in w_keys:
                    quant(key)
                for (s, e) in tiles:
                    mx_pe(s, e, 0, NT)
                lora_mm(0)
                for s in later:
                    lora_mm(s)
                for (s, e) in tiles:
                    mx_out(s, e, 0, NT)
            else:
                if len(group) == 1:
                    for key in w_keys:
                        quant(key)
                for key in sorted(V_PC_MID):
                    if V_PC_MID[key] == group[0]:
                        precopy(key, True)
                for i in range(len(tiles)):
                    if len(group) > 1 and i < len(w_keys):
                        quant(w_keys[i])
                    mx(tiles[i][0], tiles[i][1])
                    if i == 0:
                        for key in sorted(V_PC_END):
                            if V_PC_END[key] == group[0]:
                                precopy(key, True)
                for s in later:
                    lora_mm(s)
